import numpy as np
import ml_dtypes


def mxq(x, axis, fmt="e4m3"):
    dtype, down = {"e4m3": (ml_dtypes.float8_e4m3fn, 7), "e5m2": (ml_dtypes.float8_e5m2, 14)}[fmt]
    v = np.moveaxis(np.asarray(x, np.float32).astype(ml_dtypes.bfloat16).astype(np.float64), axis, -1)
    blocks = v.reshape(v.shape[:-1] + (-1, 32))
    amax = np.abs(blocks).max(-1, keepdims=True)
    byte = np.maximum(np.where(amax > 0, np.frexp(amax)[1] - 1 + 127, 0) - down, 1)
    scale = np.exp2(byte - 127.0)
    codes = (blocks / scale).astype(np.float32).astype(dtype).astype(np.float64)
    return np.moveaxis((codes * scale).reshape(v.shape), -1, axis)


WIDE = False


def mx_kscale(k):
    if not WIDE:
        return np.ones(k)
    levels = np.array([10, -10, 5, -5, 0])
    if k % 512:
        return np.exp2(np.random.permutation(np.resize(levels, k // 32))).repeat(32)
    a = np.empty((k // 512, 16))
    for p in range(k // 512):
        a[p, :8] = np.random.permutation(np.resize(levels, 8))
        for g in range(8):
            far = levels[np.abs(levels - a[p, g]) >= 10]
            a[p, g + 8] = far[np.random.randint(len(far))]
    return np.exp2(a.ravel()).repeat(32)


BF16 = ml_dtypes.bfloat16


def bf(x):
    return np.asarray(x, np.float32).astype(BF16)


def f64(x):
    return np.asarray(x).astype(np.float64)


N, IN_F, OUT_F = 1024, 512, 512
POW = 2


def setup_inputs():
    s = mx_kscale(IN_F)
    u = np.exp2(np.round(np.log2(mx_kscale(N)) / 2))
    return {"input": bf(np.random.standard_normal((N, IN_F)) * s / (u * u)[:, None]),
            "adj": bf(np.random.uniform(0.0, 1.0, (N, N)) * 1.5 / N ** 0.25 * u),
            "weight": bf(np.random.uniform(-1.0, 1.0, (IN_F, OUT_F)) * 1.7 / np.sqrt(IN_F) / s[:, None]),
            "bias": bf(np.random.standard_normal(OUT_F) * 0.3)}


def reference(input, adj, weight, bias):
    k_adj = f64(adj) ** POW
    support = mxq(f64(input), 1, "e4m3") @ mxq(f64(weight), 0, "e4m3")
    out = (mxq(k_adj, 1, "e4m3") @ mxq(support, 0, "e4m3")) + f64(bias)
    return np.where(out > 0, out, np.expm1(out))

@@ -1,0 +1,263 @@
+from contextlib import ExitStack
+
+import concourse.mybir as mybir
+from concourse.masks import make_identity
+
+F32 = mybir.dt.float32
+BF16 = mybir.dt.bfloat16
+U32 = mybir.dt.uint32
+U8 = mybir.dt.uint8
+I32 = mybir.dt.int32
+FP8X4 = mybir.dt.float8_e4m3fn_x4
+ALU = mybir.AluOpType
+ACT = mybir.ActivationFunctionType
+
+P = 128
+NODES = 1024
+IN_F = 512
+OUT_F = 512
+FLOPS = 2 * NODES * IN_F * OUT_F + 2 * NODES * NODES * OUT_F
+
+PINNED = True
+LOADS = ["W","X0","X1","X2","X3","A0","A1","A2","A3","A4","A5","A6","A7"]
+ORDER = ["RW0","TX0","RW1","EX0","TX1","QW0","QW1","EX1","TX2","QX0","TX3","EX2","QX1","BM","TA0","EX3","QX2","M1_00","BE","M1_01","QX3","TA1","ES_00","SQ0","M1_02","ES_01","M1_03","M1_11","ES_02","TA2","SQ1","M1_10","ES_03","M1_12","TA3","QK0","ES_11","ES_10","M1_13","TA4","SQ2","ES_12","TA5","TA6","QK1","ES_13","SQ3","TA7","QS0","QS1","SQ4","QK2","M2_0","QK3","SQ5","M2_1","QK4","A0","M2_2","A1","SQ6","M2_3","QK5","M2_4","A2","M2_5","X0","QK6","A3","SQ7","M2_6","C0","X1","QK7","D0","X2","M2_7","A4","C1","ST0","X3","A5","C2","X4","A6","X5","C3","A7","C4","D1","X6","D2","ST1","C5","D3","ST2","X7","D4","ST3","C6","D5","ST4","C7","D6","ST5","D7","ST6","ST7"]
+X_ENG = ["ACT","ACT","ACT","ACT"]
+S_ENG = ["DVE","DVE","DVE","DVE","DVE","ACT","DVE","DVE"]
+B_ENG = "ACT"
+K_ENG = ["ACT","ACT","ACT","ACT","ACT","ACT","ACT","ACT"]
+FORM = [3,3,3,3,2,2,2,2]
+
+
+def tile_netgraphconvolution_kernel(tc, x_in, adj, weight, bias, out):
+    nc = tc.nc
+    with ExitStack() as ctx:
+        keep = ctx.enter_context(tc.tile_pool(name="keep", bufs=1))
+        psum = ctx.enter_context(tc.psum_pool(name="psum", bufs=8))
+        banks = {}
+
+        def bank(key):
+            t = psum.tile([P, 512], F32, name="bank", tag="bank")
+            banks[key] = t
+            return t
+
+        def copy_on(eng, dst, src):
+            if eng == "ACT":
+                nc.scalar.copy(out=dst, in_=src)
+            else:
+                nc.vector.tensor_copy(out=dst, in_=src)
+
+        ident = keep.tile([P, P], F32, name="ident")
+        warm = keep.tile([P, 1], F32, name="warm")
+        ones = keep.tile([P, P], BF16, name="ones")
+        brow = keep.tile([P, OUT_F], BF16, name="brow")
+
+        x_view = x_in.rearrange("(g p h e) k -> g h p (e k)", g=2, p=P, h=2, e=2)
+        x_sb = [keep.tile([P, 2 * IN_F], BF16, name="x_sb%d" % a) for a in range(4)]
+        w_sb = keep.tile([P, 4, OUT_F], BF16, name="w_sb")
+        a_view = adj.rearrange("(m p) j -> m p j", p=P)
+        a_sb = [keep.tile([P, NODES], BF16, name="a_sb%d" % m) for m in range(8)]
+        o_view = out.rearrange("(m p) f -> m p f", p=P)
+        w_view = weight.rearrange("(p t) c -> p (t c)", t=4)
+        def head():
+            nc.vector.memset(brow[:].bitcast(I32), 0)
+            nc.scalar.dma_start(out=brow[0:1, :], in_=bias.rearrange("(o f) -> o f", o=1))
+            for ld in LOADS:
+                i = int(ld[1:]) if len(ld) > 1 else 0
+                if ld == "W":
+                    nc.sync.dma_start(
+                        out=w_sb[:].rearrange("p t c -> p (t c)"), in_=w_view
+                    )
+                elif ld[0] == "X":
+                    nc.sync.dma_start(out=x_sb[i][:], in_=x_view[i // 2, i % 2])
+                else:
+                    nc.sync.dma_start(out=a_sb[i][:], in_=a_view[i])
+
+            make_identity(nc, ident[:])
+            nc.vector.memset(ones[:], 1.0)
+            nc.vector.memset(warm[:], 0.0)
+            nc.scalar.activation(out=warm[:], in_=warm[:], func=ACT.Exp)
+
+        w_grp = keep.tile([P, OUT_F, 4], BF16, name="w_grp", align_bytes=64)
+        w_cod = keep.tile([P, OUT_F], U32, name="w_cod", align_bytes=64)
+        w_scl = keep.tile([P, OUT_F], U8, name="w_scl", align_bytes=64)
+        x_grp = [keep.tile([P, 1024], BF16, name="x_grp%d" % a, align_bytes=64) for a in range(4)]
+        x_cod = [keep.tile([P, 256], U32, name="x_cod%d" % a, align_bytes=64) for a in range(4)]
+        x_scl = [keep.tile([P, 256], U8, name="x_scl%d" % a, align_bytes=64) for a in range(4)]
+        s_grp = [keep.tile([P, 2048], BF16, name="s_grp%d" % g, align_bytes=64) for g in range(2)]
+        s_cod = [keep.tile([P, 512], U32, name="s_cod%d" % g, align_bytes=64) for g in range(2)]
+        s_scl = [keep.tile([P, 512], U8, name="s_scl%d" % g, align_bytes=64) for g in range(2)]
+        k_raw = [keep.tile([P, 1024], BF16, name="k_raw%d" % m, align_bytes=64) for m in range(8)]
+        k_grp = [keep.tile([P, 1024], BF16, name="k_grp%d" % m, align_bytes=64) for m in range(8)]
+        k_cod = [keep.tile([P, 256], U32, name="k_cod%d" % m, align_bytes=64) for m in range(8)]
+        k_scl = [keep.tile([P, 256], U8, name="k_scl%d" % m, align_bytes=64) for m in range(8)]
+        bias_sb = keep.tile([P, OUT_F], F32, name="bias_sb")
+        v = [keep.tile([P, OUT_F], F32, name="v%d" % m) for m in range(8)]
+        ex = [keep.tile([P, OUT_F], F32, name="ex%d" % m) for m in range(8)]
+
+        def op_rw(h):
+            cols = slice(h * 256, (h + 1) * 256)
+            nc.vector.tensor_copy(
+                out=w_grp[:, cols, :].rearrange("p (c i) t -> p c t i", i=4),
+                in_=w_sb[:, :, cols].rearrange("p t (c i) -> p c t i", i=4),
+            )
+
+        def op_qw(h):
+            cols = slice(h * 256, (h + 1) * 256)
+            nc.vector.quantize_mx(
+                out=w_cod[:, cols].bitcast(FP8X4),
+                scales=w_scl[:, cols],
+                in_=w_grp[:, cols, :].rearrange("p c t -> p (c t)"),
+            )
+
+        def op_tx(a):
+            xt = bank("X%d" % a)
+            xf = x_sb[a][:].bitcast(F32)
+            for u in range(2):
+                for e in range(2):
+                    nc.tensor.transpose(
+                        xt[:, (2 * u + e) * P : (2 * u + e + 1) * P],
+                        xf[:, e * 256 + u : (e + 1) * 256 : 2],
+                        ident[:],
+                    )
+
+        def op_ex(a):
+            copy_on(
+                X_ENG[a],
+                x_grp[a][:].bitcast(F32).rearrange("p (n u) -> p n u", u=2),
+                banks["X%d" % a][:].rearrange("p (u n) -> p n u", u=2),
+            )
+
+        def op_qx(a):
+            nc.vector.quantize_mx(
+                out=x_cod[a][:].bitcast(FP8X4), scales=x_scl[a][:], in_=x_grp[a][:]
+            )
+
+        def op_bm():
+            nc.tensor.matmul(out=bank("B")[:], lhsT=ones[:], rhs=brow[:], start=True, stop=True)
+
+        def op_be():
+            copy_on(B_ENG, bias_sb[:], banks["B"][:])
+
+        def op_m1(g, c):
+            sp = bank("S%d%d" % (g, c))
+            for t in range(4):
+                a, e = 2 * g + t // 2, t % 2
+                nc.tensor.matmul_mx(
+                    out=sp[:, t * P : (t + 1) * P],
+                    lhsT=x_cod[a][:, e * P : (e + 1) * P].bitcast(FP8X4),
+                    lhsT_scale=x_scl[a][:, e * P : (e + 1) * P],
+                    rhs=w_cod[:, c * P : (c + 1) * P].bitcast(FP8X4),
+                    rhs_scale=w_scl[:, c * P : (c + 1) * P],
+                    start=True,
+                    stop=True,
+                )
+
+        def op_es(g, c):
+            copy_on(
+                S_ENG[4 * g + c],
+                s_grp[g][:, c * 512 : (c + 1) * 512].rearrange("p (f t) -> p f t", t=4),
+                banks["S%d%d" % (g, c)][:].rearrange("p (t f) -> p f t", t=4),
+            )
+
+        def op_qs(g):
+            nc.vector.quantize_mx(
+                out=s_cod[g][:].bitcast(FP8X4), scales=s_scl[g][:], in_=s_grp[g][:]
+            )
+
+        def op_ta(m):
+            at = bank("A%d" % m)
+            af = a_sb[m][:].bitcast(F32)
+            for g in range(2):
+                for u in range(2):
+                    nc.tensor.transpose(
+                        at[:, (2 * u + g) * P : (2 * u + g + 1) * P],
+                        af[:, g * 256 + u : (g + 1) * 256 : 2],
+                        ident[:],
+                    )
+
+        def op_ck(m):
+            nc.vector.tensor_copy(
+                out=k_raw[m][:].bitcast(F32).rearrange("p (q u) -> p q u", u=2),
+                in_=banks["A%d" % m][:].rearrange("p (u q) -> p q u", u=2),
+            )
+
+        def op_sq(m):
+            if K_ENG[m] == "ACT":
+                nc.scalar.activation(
+                    out=k_grp[m][:].rearrange("p (q u e) -> p q u e", u=2, e=2),
+                    in_=banks["A%d" % m][:].bitcast(BF16).rearrange("p (u q e) -> p q u e", u=2, e=2),
+                    func=ACT.Square,
+                )
+            else:
+                nc.vector.tensor_tensor(out=k_grp[m][:], in0=k_raw[m][:], in1=k_raw[m][:], op=ALU.mult)
+
+        def op_qk(m):
+            nc.vector.quantize_mx(
+                out=k_cod[m][:].bitcast(FP8X4), scales=k_scl[m][:], in_=k_grp[m][:]
+            )
+
+        def op_m2(m):
+            acc = bank("O%d" % m)
+            for g in range(2):
+                nc.tensor.matmul_mx(
+                    out=acc[:],
+                    lhsT=k_cod[m][:, g * P : (g + 1) * P].bitcast(FP8X4),
+                    lhsT_scale=k_scl[m][:, g * P : (g + 1) * P],
+                    rhs=s_cod[g][:].bitcast(FP8X4),
+                    rhs_scale=s_scl[g][:],
+                    start=(g == 0),
+                    stop=(g == 1),
+                )
+
+        def op_a(m):
+            nc.vector.tensor_tensor(out=v[m][:], in0=banks["O%d" % m][:], in1=bias_sb[:], op=ALU.add)
+
+        def op_x(m):
+            nc.scalar.activation(out=ex[m][:], in_=v[m][:], func=ACT.Exp)
+
+        def op_c(m):
+            if FORM[m] == 1:
+                nc.vector.tensor_scalar(
+                    out=ex[m][:], in0=ex[m][:], scalar1=-1.0, scalar2=None, op0=ALU.add
+                )
+            elif FORM[m] == 2:
+                nc.scalar.activation(out=ex[m][:], in_=ex[m][:], func=ACT.Identity, bias=-1.0, scale=1.0)
+            else:
+                nc.gpsimd.tensor_scalar(
+                    out=ex[m][:], in0=ex[m][:], scalar1=-1.0, scalar2=1.0, op0=ALU.add, op1=ALU.mult
+                )
+
+        def op_d(m):
+            nc.vector.scalar_tensor_tensor(
+                out=v[m][:], in0=v[m][:], scalar=0.0, in1=ex[m][:], op0=ALU.max, op1=ALU.min
+            )
+
+        def op_st(m):
+            nc.sync.dma_start(out=o_view[m], in_=v[m][:])
+
+        one = {"RW": op_rw, "QW": op_qw, "TX": op_tx, "EX": op_ex, "QX": op_qx, "QS": op_qs,
+               "TA": op_ta, "CK": op_ck, "SQ": op_sq, "QK": op_qk, "A": op_a, "X": op_x,
+               "C": op_c, "D": op_d, "ST": op_st}
+
+        def emit():
+            for name in ORDER:
+                if name == "BM":
+                    op_bm()
+                elif name == "BE":
+                    op_be()
+                elif name[:3] == "M1_":
+                    op_m1(int(name[3]), int(name[4]))
+                elif name[:3] == "ES_":
+                    op_es(int(name[3]), int(name[4]))
+                elif name[:3] == "M2_":
+                    op_m2(int(name[3]))
+                else:
+                    one[name[:-1]](int(name[-1]))
+
+        if PINNED:
+            with tc.manual_schedule():
+                head()
+                emit()
+        else:
+            head()
+            emit()

@@ -7,7 +7,6 @@ F32 = mybir.dt.float32
 BF16 = mybir.dt.bfloat16
 U32 = mybir.dt.uint32
 U8 = mybir.dt.uint8
-I32 = mybir.dt.int32
 FP8X4 = mybir.dt.float8_e4m3fn_x4
 ALU = mybir.AluOpType
 ACT = mybir.ActivationFunctionType
@@ -20,10 +19,9 @@ FLOPS = 2 * NODES * IN_F * OUT_F + 2 * NODES * NODES * OUT_F
 
 PINNED = True
 LOADS = ["W","X0","X1","X2","X3","A0","A1","A2","A3","A4","A5","A6","A7"]
-ORDER = ["RW0","TX0","RW1","EX0","TX1","QW0","QW1","EX1","TX2","QX0","TX3","EX2","QX1","BM","TA0","EX3","QX2","M1_00","BE","M1_01","QX3","TA1","ES_00","SQ0","M1_02","ES_01","M1_03","M1_11","ES_02","TA2","SQ1","M1_10","ES_03","M1_12","TA3","QK0","ES_11","ES_10","M1_13","TA4","SQ2","ES_12","TA5","TA6","QK1","ES_13","SQ3","TA7","QS0","QS1","SQ4","QK2","M2_0","QK3","SQ5","M2_1","QK4","A0","M2_2","A1","SQ6","M2_3","QK5","M2_4","A2","M2_5","X0","QK6","A3","SQ7","M2_6","C0","X1","QK7","D0","X2","M2_7","A4","C1","ST0","X3","A5","C2","X4","A6","X5","C3","A7","C4","D1","X6","D2","ST1","C5","D3","ST2","X7","D4","ST3","C6","D5","ST4","C7","D6","ST5","D7","ST6","ST7"]
+ORDER = ["RW0","TX0","RW1","EX0","TX1","QW0","QW1","EX1","TX2","QX0","TX3","EX2","QX1","TA0","EX3","QX2","M1_00","M1_01","QX3","TA1","ES_00","SQ0","M1_02","ES_01","M1_03","M1_11","ES_02","TA2","SQ1","M1_10","ES_03","M1_12","TA3","QK0","ES_11","ES_10","M1_13","TA4","SQ2","ES_12","TA5","TA6","QK1","ES_13","SQ3","TA7","QS0","QS1","SQ4","QK2","M2_0","QK3","SQ5","M2_1","QK4","A0","M2_2","A1","SQ6","M2_3","QK5","M2_4","A2","M2_5","X0","QK6","A3","SQ7","M2_6","C0","X1","QK7","D0","X2","M2_7","A4","C1","ST0","X3","A5","C2","X4","A6","X5","C3","A7","C4","D1","X6","D2","ST1","C5","D3","ST2","X7","D4","ST3","C6","D5","ST4","C7","D6","ST5","D7","ST6","ST7"]
 X_ENG = ["ACT","ACT","ACT","ACT"]
 S_ENG = ["DVE","DVE","DVE","DVE","DVE","ACT","DVE","DVE"]
-B_ENG = "ACT"
 K_ENG = ["ACT","ACT","ACT","ACT","ACT","ACT","ACT","ACT"]
 FORM = [3,3,3,3,2,2,2,2]
 
@@ -48,8 +46,8 @@ def tile_netgraphconvolution_kernel(tc, x_in, adj, weight, bias, out):
 
         ident = keep.tile([P, P], F32, name="ident")
         warm = keep.tile([P, 1], F32, name="warm")
-        ones = keep.tile([P, P], BF16, name="ones")
-        brow = keep.tile([P, OUT_F], BF16, name="brow")
+        zeros = keep.tile([P, 512], BF16, name="zeros")
+        bias_sb = keep.tile([P, OUT_F], BF16, name="bias_sb")
 
         x_view = x_in.rearrange("(g p h e) k -> g h p (e k)", g=2, p=P, h=2, e=2)
         x_sb = [keep.tile([P, 2 * IN_F], BF16, name="x_sb%d" % a) for a in range(4)]
@@ -59,8 +57,6 @@ def tile_netgraphconvolution_kernel(tc, x_in, adj, weight, bias, out):
         o_view = out.rearrange("(m p) f -> m p f", p=P)
         w_view = weight.rearrange("(p t) c -> p (t c)", t=4)
         def head():
-            nc.vector.memset(brow[:].bitcast(I32), 0)
-            nc.scalar.dma_start(out=brow[0:1, :], in_=bias.rearrange("(o f) -> o f", o=1))
             for ld in LOADS:
                 i = int(ld[1:]) if len(ld) > 1 else 0
                 if ld == "W":
@@ -72,10 +68,14 @@ def tile_netgraphconvolution_kernel(tc, x_in, adj, weight, bias, out):
                 else:
                     nc.sync.dma_start(out=a_sb[i][:], in_=a_view[i])
 
+            nc.sync.dma_start(out=bias_sb[:], in_=bias.partition_broadcast(P))
+            nc.vector.memset(zeros[:], 0.0)
             make_identity(nc, ident[:])
-            nc.vector.memset(ones[:], 1.0)
             nc.vector.memset(warm[:], 0.0)
             nc.scalar.activation(out=warm[:], in_=warm[:], func=ACT.Exp)
+            bank("busy")
+            for i in range(6):
+                op_busy()
 
         w_grp = keep.tile([P, OUT_F, 4], BF16, name="w_grp", align_bytes=64)
         w_cod = keep.tile([P, OUT_F], U32, name="w_cod", align_bytes=64)
@@ -90,9 +90,11 @@ def tile_netgraphconvolution_kernel(tc, x_in, adj, weight, bias, out):
         k_grp = [keep.tile([P, 1024], BF16, name="k_grp%d" % m, align_bytes=64) for m in range(8)]
         k_cod = [keep.tile([P, 256], U32, name="k_cod%d" % m, align_bytes=64) for m in range(8)]
         k_scl = [keep.tile([P, 256], U8, name="k_scl%d" % m, align_bytes=64) for m in range(8)]
-        bias_sb = keep.tile([P, OUT_F], F32, name="bias_sb")
         v = [keep.tile([P, OUT_F], F32, name="v%d" % m) for m in range(8)]
         ex = [keep.tile([P, OUT_F], F32, name="ex%d" % m) for m in range(8)]
+
+        def op_busy():
+            nc.tensor.matmul(out=banks["busy"][:], lhsT=zeros[:, :P], rhs=zeros[:], start=True, stop=True)
 
         def op_rw(h):
             cols = slice(h * 256, (h + 1) * 256)
@@ -119,6 +121,8 @@ def tile_netgraphconvolution_kernel(tc, x_in, adj, weight, bias, out):
                         xf[:, e * 256 + u : (e + 1) * 256 : 2],
                         ident[:],
                     )
+            if a < 3:
+                op_busy()
 
         def op_ex(a):
             copy_on(
@@ -131,12 +135,6 @@ def tile_netgraphconvolution_kernel(tc, x_in, adj, weight, bias, out):
             nc.vector.quantize_mx(
                 out=x_cod[a][:].bitcast(FP8X4), scales=x_scl[a][:], in_=x_grp[a][:]
             )
-
-        def op_bm():
-            nc.tensor.matmul(out=bank("B")[:], lhsT=ones[:], rhs=brow[:], start=True, stop=True)
-
-        def op_be():
-            copy_on(B_ENG, bias_sb[:], banks["B"][:])
 
         def op_m1(g, c):
             sp = bank("S%d%d" % (g, c))
@@ -241,11 +239,7 @@ def tile_netgraphconvolution_kernel(tc, x_in, adj, weight, bias, out):
 
         def emit():
             for name in ORDER:
-                if name == "BM":
-                    op_bm()
-                elif name == "BE":
-                    op_be()
-                elif name[:3] == "M1_":
+                if name[:3] == "M1_":
                     op_m1(int(name[3]), int(name[4]))
                 elif name[:3] == "ES_":
                     op_es(int(name[3]), int(name[4]))

@@ -19,11 +19,14 @@ FLOPS = 2 * NODES * IN_F * OUT_F + 2 * NODES * NODES * OUT_F
 
 PINNED = True
 LOADS = ["W","X0","X1","X2","X3","A0","A1","A2","A3","A4","A5","A6","A7"]
-ORDER = ["RW0","TX0","RW1","EX0","TX1","QW0","QW1","EX1","TX2","QX0","TX3","EX2","QX1","TA0","EX3","QX2","M1_00","M1_01","QX3","TA1","ES_00","SQ0","M1_02","ES_01","M1_03","M1_11","ES_02","TA2","SQ1","M1_10","ES_03","M1_12","TA3","QK0","ES_11","ES_10","M1_13","TA4","SQ2","ES_12","TA5","TA6","QK1","ES_13","SQ3","TA7","QS0","QS1","SQ4","QK2","M2_0","QK3","SQ5","M2_1","QK4","A0","M2_2","A1","SQ6","M2_3","QK5","M2_4","A2","M2_5","X0","QK6","A3","SQ7","M2_6","C0","X1","QK7","D0","X2","M2_7","A4","C1","ST0","X3","A5","C2","X4","A6","X5","C3","A7","C4","D1","X6","D2","ST1","C5","D3","ST2","X7","D4","ST3","C6","D5","ST4","C7","D6","ST5","D7","ST6","ST7"]
+ORDER = ["RW0","RW1","TX0","QW0","TX1","QW1","EX0","TX2","EX1","QX0","TX3","SN0","EX2","QX1","EX3","TB0","SN1","M1_00","SE0","QX2","M1_01","QX3","M1_02","ES_00","SN2","M1_03","ES_01","TB1","QK0","TB2","ES_02","SN3","M1_10","ES_03","SE2","M1_11","M1_12","ES_10","M1_13","ES_12","ES_11","TB3","ES_13","TA4","SE1","QS0","SQ4","TA5","QS1","TA6","QK1","SQ5","M2_0","QK2","SE3","M2_1","SQ6","A0","TA7","QK3","A1","M2_2","SQ7","QK4","M2_3","A2","M2_4","X0","A3","X1","QK5","A4","C0","X2","M2_5","X3","QK6","A5","C1","M2_6","X4","QK7","C3","D0","M2_7","X5","A6","C2","ST0","C4","A7","X6","D1","C5","D2","ST1","X7","D3","ST2","C6","D4","ST3","C7","D5","ST4","D6","ST5","D7","ST6","ST7"]
 X_ENG = ["ACT","ACT","ACT","ACT"]
-S_ENG = ["DVE","DVE","DVE","DVE","DVE","ACT","DVE","DVE"]
-K_ENG = ["ACT","ACT","ACT","ACT","ACT","ACT","ACT","ACT"]
-FORM = [3,3,3,3,2,2,2,2]
+S_ENG = ["ACT","ACT","ACT","ACT","ACT","ACT","DVE","DVE"]
+K_ENG = ["ACT","ACT","DVE","DVE","ACT","ACT","ACT","ACT"]
+W_ENG = ["DVE","ACT"]
+BUSY = [1,0,1,0]
+FRONT = 6
+FORM = [3,3,3,2,2,2,2,2]
 
 
 def tile_netgraphconvolution_kernel(tc, x_in, adj, weight, bias, out):
@@ -74,7 +77,7 @@ def tile_netgraphconvolution_kernel(tc, x_in, adj, weight, bias, out):
             nc.vector.memset(warm[:], 0.0)
             nc.scalar.activation(out=warm[:], in_=warm[:], func=ACT.Exp)
             bank("busy")
-            for i in range(6):
+            for i in range(FRONT):
                 op_busy()
 
         w_grp = keep.tile([P, OUT_F, 4], BF16, name="w_grp", align_bytes=64)
@@ -98,9 +101,10 @@ def tile_netgraphconvolution_kernel(tc, x_in, adj, weight, bias, out):
 
         def op_rw(h):
             cols = slice(h * 256, (h + 1) * 256)
-            nc.vector.tensor_copy(
-                out=w_grp[:, cols, :].rearrange("p (c i) t -> p c t i", i=4),
-                in_=w_sb[:, :, cols].rearrange("p t (c i) -> p c t i", i=4),
+            copy_on(
+                W_ENG[h],
+                w_grp[:, cols, :].rearrange("p (c i) t -> p c t i", i=4),
+                w_sb[:, :, cols].rearrange("p t (c i) -> p c t i", i=4),
             )
 
         def op_qw(h):
@@ -121,7 +125,7 @@ def tile_netgraphconvolution_kernel(tc, x_in, adj, weight, bias, out):
                         xf[:, e * 256 + u : (e + 1) * 256 : 2],
                         ident[:],
                     )
-            if a < 3:
+            for i in range(BUSY[a]):
                 op_busy()
 
         def op_ex(a):
@@ -173,21 +177,34 @@ def tile_netgraphconvolution_kernel(tc, x_in, adj, weight, bias, out):
                         ident[:],
                     )
 
-        def op_ck(m):
-            nc.vector.tensor_copy(
-                out=k_raw[m][:].bitcast(F32).rearrange("p (q u) -> p q u", u=2),
-                in_=banks["A%d" % m][:].rearrange("p (u q) -> p q u", u=2),
+        def op_sn(m):
+            adj_words = a_sb[m][:].rearrange("p (q u e) -> p u q e", u=2, e=2)
+            nc.vector.tensor_tensor(
+                out=k_raw[m][:].rearrange("p (u q e) -> p u q e", u=2, e=2),
+                in0=adj_words, in1=adj_words, op=ALU.mult,
+            )
+
+        def op_tb(m):
+            at = bank("A%d" % m)
+            kf = k_raw[m][:].bitcast(F32)
+            for u in range(2):
+                for g in range(2):
+                    cols = slice((2 * u + g) * P, (2 * u + g + 1) * P)
+                    nc.tensor.transpose(at[:, cols], kf[:, cols], ident[:])
+
+        def op_se(m):
+            copy_on(
+                K_ENG[m],
+                k_grp[m][:].bitcast(F32).rearrange("p (q u) -> p q u", u=2),
+                banks["A%d" % m][:].rearrange("p (u q) -> p q u", u=2),
             )
 
         def op_sq(m):
-            if K_ENG[m] == "ACT":
-                nc.scalar.activation(
-                    out=k_grp[m][:].rearrange("p (q u e) -> p q u e", u=2, e=2),
-                    in_=banks["A%d" % m][:].bitcast(BF16).rearrange("p (u q e) -> p q u e", u=2, e=2),
-                    func=ACT.Square,
-                )
-            else:
-                nc.vector.tensor_tensor(out=k_grp[m][:], in0=k_raw[m][:], in1=k_raw[m][:], op=ALU.mult)
+            nc.scalar.activation(
+                out=k_grp[m][:].rearrange("p (q u e) -> p q u e", u=2, e=2),
+                in_=banks["A%d" % m][:].bitcast(BF16).rearrange("p (u q e) -> p q u e", u=2, e=2),
+                func=ACT.Square,
+            )
 
         def op_qk(m):
             nc.vector.quantize_mx(
@@ -234,7 +251,7 @@ def tile_netgraphconvolution_kernel(tc, x_in, adj, weight, bias, out):
             nc.sync.dma_start(out=o_view[m], in_=v[m][:])
 
         one = {"RW": op_rw, "QW": op_qw, "TX": op_tx, "EX": op_ex, "QX": op_qx, "QS": op_qs,
-               "TA": op_ta, "CK": op_ck, "SQ": op_sq, "QK": op_qk, "A": op_a, "X": op_x,
+               "TA": op_ta, "TB": op_tb, "SN": op_sn, "SE": op_se, "SQ": op_sq, "QK": op_qk, "A": op_a, "X": op_x,
                "C": op_c, "D": op_d, "ST": op_st}
 
         def emit():

@@ -19,12 +19,12 @@ FLOPS = 2 * NODES * IN_F * OUT_F + 2 * NODES * NODES * OUT_F
 
 PINNED = True
 LOADS = ["W","X0","X1","X2","X3","A0","A1","A2","A3","A4","A5","A6","A7"]
-ORDER = ["RW0","RW1","TX0","QW0","TX1","QW1","EX0","TX2","EX1","QX0","TX3","SN0","EX2","QX1","EX3","TB0","SN1","M1_00","SE0","QX2","M1_01","QX3","M1_02","ES_00","SN2","M1_03","ES_01","TB1","QK0","TB2","ES_02","SN3","M1_10","ES_03","SE2","M1_11","M1_12","ES_10","M1_13","ES_12","ES_11","TB3","ES_13","TA4","SE1","QS0","SQ4","TA5","QS1","TA6","QK1","SQ5","M2_0","QK2","SE3","M2_1","SQ6","A0","TA7","QK3","A1","M2_2","SQ7","QK4","M2_3","A2","M2_4","X0","A3","X1","QK5","A4","C0","X2","M2_5","X3","QK6","A5","C1","M2_6","X4","QK7","C3","D0","M2_7","X5","A6","C2","ST0","C4","A7","X6","D1","C5","D2","ST1","X7","D3","ST2","C6","D4","ST3","C7","D5","ST4","D6","ST5","D7","ST6","ST7"]
+ORDER = ["RW0","RW1","TX0","QW0","TX1","QW1","EX0","TX2","EX1","QX0","TX3","SN0","EX2","QX1","EX3","TB0","SN1","M1_00","SE0","QX2","M1_01","QX3","M1_02","ES_00","SN2","M1_03","ES_01","M1_10","QK0","M1_11","ES_02","SN3","M1_12","M1_13","ES_03","ES_12","TB1","ES_10","ES_13","TB2","TB3","ES_11","SE2","TA4","SE1","QS0","TA5","SQ4","TA6","QS1","TA7","QK1","QK2","SQ5","M2_0","SE3","M2_1","A0","SQ6","M2_2","QK3","A1","M2_3","SQ7","QK4","A2","M2_4","X0","A3","X1","QK5","A4","C0","M2_5","X2","QK6","X3","A5","C1","M2_6","X4","QK7","C3","D0","M2_7","X5","A6","C2","ST0","C4","A7","X6","D1","C5","D2","ST1","X7","D3","ST2","C6","D4","ST3","C7","D5","ST4","D6","ST5","D7","ST6","ST7"]
 X_ENG = ["ACT","ACT","ACT","ACT"]
 S_ENG = ["ACT","ACT","ACT","ACT","ACT","ACT","DVE","DVE"]
 K_ENG = ["ACT","ACT","DVE","DVE","ACT","ACT","ACT","ACT"]
 W_ENG = ["DVE","ACT"]
-BUSY = [1,0,1,0]
+BUSY = [1,0,1,1]
 FRONT = 6
 FORM = [3,3,3,2,2,2,2,2]
 

@@ -19,10 +19,10 @@ FLOPS = 2 * NODES * IN_F * OUT_F + 2 * NODES * NODES * OUT_F
 
 PINNED = True
 LOADS = ["W","X0","X1","X2","X3","A0","A1","A2","A3","A4","A5","A6","A7"]
-ORDER = ["RW0","RW1","TX0","QW0","TX1","QW1","EX0","TX2","EX1","QX0","TX3","SN0","EX2","QX1","EX3","TB0","SN1","M1_00","SE0","QX2","M1_01","QX3","M1_02","ES_00","SN2","M1_03","ES_01","M1_10","QK0","M1_11","ES_02","SN3","M1_12","M1_13","ES_03","ES_12","TB1","ES_10","ES_13","TB2","TB3","ES_11","SE2","TA4","SE1","QS0","TA5","SQ4","TA6","QS1","TA7","QK1","QK2","SQ5","M2_0","SE3","M2_1","A0","SQ6","M2_2","QK3","A1","M2_3","SQ7","QK4","A2","M2_4","X0","A3","X1","QK5","A4","C0","M2_5","X2","QK6","X3","A5","C1","M2_6","X4","QK7","C3","D0","M2_7","X5","A6","C2","ST0","C4","A7","X6","D1","C5","D2","ST1","X7","D3","ST2","C6","D4","ST3","C7","D5","ST4","D6","ST5","D7","ST6","ST7"]
+ORDER = ["RW0","RW1","TX0","QW0","TX1","QW1","EX0","TX2","EX1","QX0","TX3","SN0","EX2","QX1","EX3","TB0","SN1","M1_00","SE0","QX2","M1_01","QX3","M1_02","ES_00","SN2","M1_03","ES_01","M1_10","QK0","M1_11","ES_02","SN3","M1_12","M1_13","ES_03","SN4","TB1","ES_10","ES_12","TB2","TB3","ES_11","ES_13","TB4","TA5","SE1","QS0","TA6","SE2","QS1","TA7","SE4","QK1","QK2","SQ5","M2_0","SE3","M2_1","A0","SQ6","M2_2","QK3","A1","M2_3","SQ7","QK4","A2","M2_4","A3","X0","QK5","X1","A4","C0","M2_5","X2","QK6","X3","A5","C1","M2_6","X4","QK7","D0","C3","M2_7","A6","C2","X5","ST0","A7","C4","D1","X6","D2","C5","ST1","D3","X7","ST2","D4","C6","ST3","D5","C7","ST4","D6","ST5","D7","ST6","ST7"]
 X_ENG = ["ACT","ACT","ACT","ACT"]
 S_ENG = ["ACT","ACT","ACT","ACT","ACT","ACT","DVE","DVE"]
-K_ENG = ["ACT","ACT","DVE","DVE","ACT","ACT","ACT","ACT"]
+K_ENG = ["ACT","ACT","ACT","DVE","ACT","ACT","ACT","ACT"]
 W_ENG = ["DVE","ACT"]
 BUSY = [1,0,1,1]
 FRONT = 6
@@ -72,7 +72,7 @@ def tile_netgraphconvolution_kernel(tc, x_in, adj, weight, bias, out):
                     nc.sync.dma_start(out=a_sb[i][:], in_=a_view[i])
 
             nc.sync.dma_start(out=bias_sb[:], in_=bias.partition_broadcast(P))
-            nc.vector.memset(zeros[:], 0.0)
+            nc.vector.memset(zeros[:].bitcast(F32), 0.0)
             make_identity(nc, ident[:])
             nc.vector.memset(warm[:], 0.0)
             nc.scalar.activation(out=warm[:], in_=warm[:], func=ACT.Exp)

@@ -178,9 +178,9 @@ def tile_netgraphconvolution_kernel(tc, x_in, adj, weight, bias, out):
                     )
 
         def op_sn(m):
-            adj_words = a_sb[m][:].rearrange("p (q u e) -> p u q e", u=2, e=2)
+            adj_words = a_sb[m][:].rearrange("p (q u e) -> p q u e", u=2, e=2)
             nc.vector.tensor_tensor(
-                out=k_raw[m][:].rearrange("p (u q e) -> p u q e", u=2, e=2),
+                out=k_raw[m][:].rearrange("p (u q e) -> p q u e", u=2, e=2),
                 in0=adj_words, in1=adj_words, op=ALU.mult,
             )
 

from contextlib import ExitStack

import concourse.mybir as mybir
from concourse.masks import make_identity

F32 = mybir.dt.float32
BF16 = mybir.dt.bfloat16
U32 = mybir.dt.uint32
U8 = mybir.dt.uint8
FP8X4 = mybir.dt.float8_e4m3fn_x4
ALU = mybir.AluOpType
ACT = mybir.ActivationFunctionType

P = 128
NODES = 1024
IN_F = 512
OUT_F = 512
FLOPS = 2 * NODES * IN_F * OUT_F + 2 * NODES * NODES * OUT_F

PINNED = True
LOADS = ["W","X0","X1","X2","X3","A0","A1","A2","A3","A4","A5","A6","A7"]
ORDER = ["RW0","RW1","TX0","QW0","TX1","QW1","EX0","TX2","EX1","QX0","TX3","SN0","EX2","QX1","EX3","TB0","SN1","M1_00","SE0","QX2","M1_01","QX3","M1_02","ES_00","SN2","M1_03","ES_01","M1_10","QK0","M1_11","ES_02","SN3","M1_12","M1_13","ES_03","SN4","TB1","ES_10","ES_12","TB2","TB3","ES_11","ES_13","TB4","TA5","SE1","QS0","TA6","SE2","QS1","TA7","SE4","QK1","QK2","SQ5","M2_0","SE3","M2_1","A0","SQ6","M2_2","QK3","A1","M2_3","SQ7","QK4","A2","M2_4","A3","X0","QK5","X1","A4","C0","M2_5","X2","QK6","X3","A5","C1","M2_6","X4","QK7","D0","C3","M2_7","A6","C2","X5","ST0","A7","C4","D1","X6","D2","C5","ST1","D3","X7","ST2","D4","C6","ST3","D5","C7","ST4","D6","ST5","D7","ST6","ST7"]
X_ENG = ["ACT","ACT","ACT","ACT"]
S_ENG = ["ACT","ACT","ACT","ACT","ACT","ACT","DVE","DVE"]
K_ENG = ["ACT","ACT","ACT","DVE","ACT","ACT","ACT","ACT"]
W_ENG = ["DVE","ACT"]
BUSY = [1,0,1,1]
FRONT = 6
FORM = [3,3,3,2,2,2,2,2]


def tile_netgraphconvolution_kernel(tc, x_in, adj, weight, bias, out):
    nc = tc.nc
    with ExitStack() as ctx:
        keep = ctx.enter_context(tc.tile_pool(name="keep", bufs=1))
        psum = ctx.enter_context(tc.psum_pool(name="psum", bufs=8))
        banks = {}

        def bank(key):
            t = psum.tile([P, 512], F32, name="bank", tag="bank")
            banks[key] = t
            return t

        def copy_on(eng, dst, src):
            if eng == "ACT":
                nc.scalar.copy(out=dst, in_=src)
            else:
                nc.vector.tensor_copy(out=dst, in_=src)

        ident = keep.tile([P, P], F32, name="ident")
        warm = keep.tile([P, 1], F32, name="warm")
        zeros = keep.tile([P, 512], BF16, name="zeros")
        bias_sb = keep.tile([P, OUT_F], BF16, name="bias_sb")

        x_view = x_in.rearrange("(g p h e) k -> g h p (e k)", g=2, p=P, h=2, e=2)
        x_sb = [keep.tile([P, 2 * IN_F], BF16, name="x_sb%d" % a) for a in range(4)]
        w_sb = keep.tile([P, 4, OUT_F], BF16, name="w_sb")
        a_view = adj.rearrange("(m p) j -> m p j", p=P)
        a_sb = [keep.tile([P, NODES], BF16, name="a_sb%d" % m) for m in range(8)]
        o_view = out.rearrange("(m p) f -> m p f", p=P)
        w_view = weight.rearrange("(p t) c -> p (t c)", t=4)
        def head():
            for ld in LOADS:
                i = int(ld[1:]) if len(ld) > 1 else 0
                if ld == "W":
                    nc.sync.dma_start(
                        out=w_sb[:].rearrange("p t c -> p (t c)"), in_=w_view
                    )
                elif ld[0] == "X":
                    nc.sync.dma_start(out=x_sb[i][:], in_=x_view[i // 2, i % 2])
                else:
                    nc.sync.dma_start(out=a_sb[i][:], in_=a_view[i])

            nc.sync.dma_start(out=bias_sb[:], in_=bias.partition_broadcast(P))
            nc.vector.memset(zeros[:].bitcast(F32), 0.0)
            make_identity(nc, ident[:])
            nc.vector.memset(warm[:], 0.0)
            nc.scalar.activation(out=warm[:], in_=warm[:], func=ACT.Exp)
            bank("busy")
            for i in range(FRONT):
                op_busy()

        w_grp = keep.tile([P, OUT_F, 4], BF16, name="w_grp", align_bytes=64)
        w_cod = keep.tile([P, OUT_F], U32, name="w_cod", align_bytes=64)
        w_scl = keep.tile([P, OUT_F], U8, name="w_scl", align_bytes=64)
        x_grp = [keep.tile([P, 1024], BF16, name="x_grp%d" % a, align_bytes=64) for a in range(4)]
        x_cod = [keep.tile([P, 256], U32, name="x_cod%d" % a, align_bytes=64) for a in range(4)]
        x_scl = [keep.tile([P, 256], U8, name="x_scl%d" % a, align_bytes=64) for a in range(4)]
        s_grp = [keep.tile([P, 2048], BF16, name="s_grp%d" % g, align_bytes=64) for g in range(2)]
        s_cod = [keep.tile([P, 512], U32, name="s_cod%d" % g, align_bytes=64) for g in range(2)]
        s_scl = [keep.tile([P, 512], U8, name="s_scl%d" % g, align_bytes=64) for g in range(2)]
        k_raw = [keep.tile([P, 1024], BF16, name="k_raw%d" % m, align_bytes=64) for m in range(8)]
        k_grp = [keep.tile([P, 1024], BF16, name="k_grp%d" % m, align_bytes=64) for m in range(8)]
        k_cod = [keep.tile([P, 256], U32, name="k_cod%d" % m, align_bytes=64) for m in range(8)]
        k_scl = [keep.tile([P, 256], U8, name="k_scl%d" % m, align_bytes=64) for m in range(8)]
        v = [keep.tile([P, OUT_F], F32, name="v%d" % m) for m in range(8)]
        ex = [keep.tile([P, OUT_F], F32, name="ex%d" % m) for m in range(8)]

        def op_busy():
            nc.tensor.matmul(out=banks["busy"][:], lhsT=zeros[:, :P], rhs=zeros[:], start=True, stop=True)

        def op_rw(h):
            cols = slice(h * 256, (h + 1) * 256)
            copy_on(
                W_ENG[h],
                w_grp[:, cols, :].rearrange("p (c i) t -> p c t i", i=4),
                w_sb[:, :, cols].rearrange("p t (c i) -> p c t i", i=4),
            )

        def op_qw(h):
            cols = slice(h * 256, (h + 1) * 256)
            nc.vector.quantize_mx(
                out=w_cod[:, cols].bitcast(FP8X4),
                scales=w_scl[:, cols],
                in_=w_grp[:, cols, :].rearrange("p c t -> p (c t)"),
            )

        def op_tx(a):
            xt = bank("X%d" % a)
            xf = x_sb[a][:].bitcast(F32)
            for u in range(2):
                for e in range(2):
                    nc.tensor.transpose(
                        xt[:, (2 * u + e) * P : (2 * u + e + 1) * P],
                        xf[:, e * 256 + u : (e + 1) * 256 : 2],
                        ident[:],
                    )
            for i in range(BUSY[a]):
                op_busy()

        def op_ex(a):
            copy_on(
                X_ENG[a],
                x_grp[a][:].bitcast(F32).rearrange("p (n u) -> p n u", u=2),
                banks["X%d" % a][:].rearrange("p (u n) -> p n u", u=2),
            )

        def op_qx(a):
            nc.vector.quantize_mx(
                out=x_cod[a][:].bitcast(FP8X4), scales=x_scl[a][:], in_=x_grp[a][:]
            )

        def op_m1(g, c):
            sp = bank("S%d%d" % (g, c))
            for t in range(4):
                a, e = 2 * g + t // 2, t % 2
                nc.tensor.matmul_mx(
                    out=sp[:, t * P : (t + 1) * P],
                    lhsT=x_cod[a][:, e * P : (e + 1) * P].bitcast(FP8X4),
                    lhsT_scale=x_scl[a][:, e * P : (e + 1) * P],
                    rhs=w_cod[:, c * P : (c + 1) * P].bitcast(FP8X4),
                    rhs_scale=w_scl[:, c * P : (c + 1) * P],
                    start=True,
                    stop=True,
                )

        def op_es(g, c):
            copy_on(
                S_ENG[4 * g + c],
                s_grp[g][:, c * 512 : (c + 1) * 512].rearrange("p (f t) -> p f t", t=4),
                banks["S%d%d" % (g, c)][:].rearrange("p (t f) -> p f t", t=4),
            )

        def op_qs(g):
            nc.vector.quantize_mx(
                out=s_cod[g][:].bitcast(FP8X4), scales=s_scl[g][:], in_=s_grp[g][:]
            )

        def op_ta(m):
            at = bank("A%d" % m)
            af = a_sb[m][:].bitcast(F32)
            for g in range(2):
                for u in range(2):
                    nc.tensor.transpose(
                        at[:, (2 * u + g) * P : (2 * u + g + 1) * P],
                        af[:, g * 256 + u : (g + 1) * 256 : 2],
                        ident[:],
                    )

        def op_sn(m):
            adj_words = a_sb[m][:].rearrange("p (q u e) -> p q u e", u=2, e=2)
            nc.vector.tensor_tensor(
                out=k_raw[m][:].rearrange("p (u q e) -> p q u e", u=2, e=2),
                in0=adj_words, in1=adj_words, op=ALU.mult,
            )

        def op_tb(m):
            at = bank("A%d" % m)
            kf = k_raw[m][:].bitcast(F32)
            for u in range(2):
                for g in range(2):
                    cols = slice((2 * u + g) * P, (2 * u + g + 1) * P)
                    nc.tensor.transpose(at[:, cols], kf[:, cols], ident[:])

        def op_se(m):
            copy_on(
                K_ENG[m],
                k_grp[m][:].bitcast(F32).rearrange("p (q u) -> p q u", u=2),
                banks["A%d" % m][:].rearrange("p (u q) -> p q u", u=2),
            )

        def op_sq(m):
            nc.scalar.activation(
                out=k_grp[m][:].rearrange("p (q u e) -> p q u e", u=2, e=2),
                in_=banks["A%d" % m][:].bitcast(BF16).rearrange("p (u q e) -> p q u e", u=2, e=2),
                func=ACT.Square,
            )

        def op_qk(m):
            nc.vector.quantize_mx(
                out=k_cod[m][:].bitcast(FP8X4), scales=k_scl[m][:], in_=k_grp[m][:]
            )

        def op_m2(m):
            acc = bank("O%d" % m)
            for g in range(2):
                nc.tensor.matmul_mx(
                    out=acc[:],
                    lhsT=k_cod[m][:, g * P : (g + 1) * P].bitcast(FP8X4),
                    lhsT_scale=k_scl[m][:, g * P : (g + 1) * P],
                    rhs=s_cod[g][:].bitcast(FP8X4),
                    rhs_scale=s_scl[g][:],
                    start=(g == 0),
                    stop=(g == 1),
                )

        def op_a(m):
            nc.vector.tensor_tensor(out=v[m][:], in0=banks["O%d" % m][:], in1=bias_sb[:], op=ALU.add)

        def op_x(m):
            nc.scalar.activation(out=ex[m][:], in_=v[m][:], func=ACT.Exp)

        def op_c(m):
            if FORM[m] == 1:
                nc.vector.tensor_scalar(
                    out=ex[m][:], in0=ex[m][:], scalar1=-1.0, scalar2=None, op0=ALU.add
                )
            elif FORM[m] == 2:
                nc.scalar.activation(out=ex[m][:], in_=ex[m][:], func=ACT.Identity, bias=-1.0, scale=1.0)
            else:
                nc.gpsimd.tensor_scalar(
                    out=ex[m][:], in0=ex[m][:], scalar1=-1.0, scalar2=1.0, op0=ALU.add, op1=ALU.mult
                )

        def op_d(m):
            nc.vector.scalar_tensor_tensor(
                out=v[m][:], in0=v[m][:], scalar=0.0, in1=ex[m][:], op0=ALU.max, op1=ALU.min
            )

        def op_st(m):
            nc.sync.dma_start(out=o_view[m], in_=v[m][:])

        one = {"RW": op_rw, "QW": op_qw, "TX": op_tx, "EX": op_ex, "QX": op_qx, "QS": op_qs,
               "TA": op_ta, "TB": op_tb, "SN": op_sn, "SE": op_se, "SQ": op_sq, "QK": op_qk, "A": op_a, "X": op_x,
               "C": op_c, "D": op_d, "ST": op_st}

        def emit():
            for name in ORDER:
                if name[:3] == "M1_":
                    op_m1(int(name[3]), int(name[4]))
                elif name[:3] == "ES_":
                    op_es(int(name[3]), int(name[4]))
                elif name[:3] == "M2_":
                    op_m2(int(name[3]))
                else:
                    one[name[:-1]](int(name[-1]))

        if PINNED:
            with tc.manual_schedule():
                head()
                emit()
        else:
            head()
            emit()
